import numpy as np
import ml_dtypes


def mxq(x, axis, fmt="e4m3"):
    dtype, down = {"e4m3": (ml_dtypes.float8_e4m3fn, 7), "e5m2": (ml_dtypes.float8_e5m2, 14)}[fmt]
    v = np.moveaxis(np.asarray(x, np.float32).astype(ml_dtypes.bfloat16).astype(np.float64), axis, -1)
    blocks = v.reshape(v.shape[:-1] + (-1, 32))
    amax = np.abs(blocks).max(-1, keepdims=True)
    byte = np.maximum(np.where(amax > 0, np.frexp(amax)[1] - 1 + 127, 0) - down, 1)
    scale = np.exp2(byte - 127.0)
    codes = (blocks / scale).astype(np.float32).astype(dtype).astype(np.float64)
    return np.moveaxis((codes * scale).reshape(v.shape), -1, axis)


WIDE = False


def mx_kscale(k):
    if not WIDE:
        return np.ones(k)
    levels = np.array([10, -10, 5, -5, 0])
    a = np.random.permutation(np.resize(levels, k // 512 * 4)).reshape(k // 512, 4)
    idx = np.arange(k)
    return np.exp2(a[idx // 512, idx % 128 // 32])


BF16 = ml_dtypes.bfloat16


def bf(x):
    return np.asarray(x, np.float32).astype(BF16)


def f64(x):
    return np.asarray(x).astype(np.float64)


E2M1 = np.array([0.0, 0.5, 1.0, 1.5, 2.0, 3.0, 4.0, 6.0, -0.0, -0.5, -1.0, -1.5, -2.0, -3.0, -4.0, -6.0])


def pack_weight(w, fmt):
    k, n = w.shape
    w = f64(bf(w)).reshape(k // 32, 32, n)
    amax = np.abs(w).max(1)
    if fmt == "e4m3":
        byte = np.frexp(amax)[1] - 1 + 127 - 7
    else:
        mant, ex = np.frexp(amax / 6.0)
        byte = np.where(mant > 0.5, ex, ex - 1) + 127
    byte = np.clip(np.where(amax > 0, byte, 1), 1, 254)
    scaled = (w * np.exp2(127.0 - byte)[:, None, :]).reshape(k, n).astype(np.float32)
    by_word = np.ascontiguousarray(scaled.reshape(k // 512, 128, 4, n).transpose(0, 1, 3, 2))
    if fmt == "e4m3":
        words = by_word.astype(ml_dtypes.float8_e4m3fn).view(np.uint8)
    else:
        c = by_word.astype(ml_dtypes.float4_e2m1fn).view(np.uint8) & 0xF
        words = c[..., 0::2] | (c[..., 1::2] << 4)
    return np.ascontiguousarray(words), np.ascontiguousarray(byte.astype(np.uint8).reshape(k // 512, 16, n))


def unpack_weight(words, scales, fmt):
    g, p, n, _ = words.shape
    if fmt == "e4m3":
        vals = np.ascontiguousarray(words).view(ml_dtypes.float8_e4m3fn).astype(np.float64)
    else:
        nib = np.empty((g, p, n, 4), np.uint8)
        nib[..., 0::2] = words & 0xF
        nib[..., 1::2] = words >> 4
        vals = E2M1[nib]
    vals = vals * np.repeat(np.exp2(scales.astype(np.float64) - 127.0), 8, axis=1)[..., None]
    return vals.transpose(0, 1, 3, 2).reshape(g * 512, n)


B, S, IN, OUT = 2, 128, 2048, 5632


def setup_inputs():
    s = mx_kscale(IN)
    x = bf(np.random.standard_normal((B, S, IN)) * s)
    w = np.random.standard_normal((IN, OUT)) * 0.022 / s[:, None]
    w_words, w_scales = pack_weight(w, "e4m3")
    return {"x": x, "w_words": w_words, "w_scales": w_scales}


def reference(x, w_words, w_scales):
    w = unpack_weight(w_words, w_scales, "e4m3")
    in_f, out_f = w.shape
    x = f64(x)
    out_shape = x.shape[:-1] + (out_f,)
    x2 = x.reshape(-1, in_f)
    out = mxq(x2, 1, "e4m3") @ w
    return out.reshape(out_shape)

@@ -1,0 +1,123 @@
+from contextlib import ExitStack
+
+import concourse.mybir as mybir
+from concourse.masks import make_identity
+
+F32 = mybir.dt.float32
+BF16 = mybir.dt.bfloat16
+I32 = mybir.dt.int32
+U32 = mybir.dt.uint32
+U8 = mybir.dt.uint8
+FP8X4 = mybir.dt.float8_e4m3fn_x4
+
+P = 128
+ROWS = 256
+K = 2048
+OUT = 5632
+PASSES = 4
+ROW_TILES = 2
+N_TILE = 512
+COLUMN_GROUPS = ((0, 2048), (2048, 2048), (4096, 1536))
+
+FLOPS = 2 * ROWS * K * OUT
+
+
+def tile_quantlinear_kernel(tc, x, w_words, w_scales, out):
+    nc = tc.nc
+    with ExitStack() as ctx:
+        keep = ctx.enter_context(tc.tile_pool(name="keep", bufs=1))
+        psum = ctx.enter_context(tc.psum_pool(name="psum", bufs=1))
+        ctx.enter_context(tc.manual_schedule())
+
+        w_planes = keep.tile([P, OUT], U8, name="w_planes", align_bytes=64)
+        nc.vector.memset(w_planes[:].bitcast(I32), 0)
+
+        ident = keep.tile([P, P], F32, name="ident")
+        make_identity(nc, ident[:])
+
+        x_sb = []
+        for m in range(ROW_TILES):
+            x_m = keep.tile([P, K], BF16, name="x_sb_%d" % m)
+            nc.sync.dma_start(out=x_m[:], in_=x[m])
+            x_sb.append(x_m)
+
+        for q in range(4):
+            nc.sync.dma_start(
+                out=w_planes[32 * q : 32 * q + 16, :].bitcast(I32),
+                in_=w_scales[:, 4 * q : 4 * q + 4, :].bitcast(I32),
+            )
+
+        w_sb = {}
+        for cg, (c0, width) in enumerate(COLUMN_GROUPS):
+            for g in range(PASSES):
+                w_t = keep.tile([P, width], U32, name="w_%d_%d" % (cg, g), align_bytes=64)
+                src = w_words[g].rearrange("p n t -> p (n t)")[:, 4 * c0 : 4 * (c0 + width)]
+                nc.sync.dma_start(out=w_t[:].bitcast(I32), in_=src.bitcast(I32))
+                w_sb[(cg, g)] = w_t
+
+        x_codes = {}
+        x_planes = {}
+        grouped = {}
+        for m in range(ROW_TILES):
+            x_words = x_sb[m][:].bitcast(F32)
+            for h in range(2):
+                xt = psum.tile([P, 2, 2, P], F32, name="xt_%d_%d" % (m, h), tag="bank%d" % (4 + 2 * m + h))
+                for gg in range(2):
+                    g = 2 * h + gg
+                    for u in range(2):
+                        nc.tensor.transpose(
+                            xt[:, gg, u, :],
+                            x_words[:, 256 * g + u : 256 * (g + 1) : 2],
+                            ident[:],
+                        )
+                grp = keep.tile([P, 4 * 2 * P], BF16, name="grouped_%d_%d" % (m, h), align_bytes=64)
+                dst = grp[:].bitcast(F32).rearrange("p (g c u) -> p g c u", g=2, c=P, u=2)
+                src = xt[:].rearrange("p g u c -> p g c u")
+                if h == 0:
+                    nc.vector.tensor_copy(out=dst, in_=src)
+                else:
+                    nc.scalar.copy(out=dst, in_=src)
+                grouped[(m, h)] = grp
+            for h in (1, 0):
+                codes = keep.tile([P, 2 * P], U32, name="x_codes_%d_%d" % (m, h), align_bytes=64)
+                plane = keep.tile([P, 2 * P], U8, name="x_plane_%d_%d" % (m, h), align_bytes=64)
+                nc.vector.quantize_mx(
+                    out=codes[:].bitcast(FP8X4),
+                    scales=plane[:],
+                    in_=grouped[(m, h)][:],
+                )
+                x_codes[(m, h)] = codes
+                x_planes[(m, h)] = plane
+
+        for cg, (c0, width) in enumerate(COLUMN_GROUPS):
+            n_tiles = width // N_TILE
+            acc = {}
+            staged = []
+            for m in range(ROW_TILES):
+                staged.append(keep.tile([P, width], F32, name="staged_%d_%d" % (cg, m)))
+            for n in range(n_tiles):
+                for m in range(ROW_TILES):
+                    acc[(n, m)] = psum.tile(
+                        [P, N_TILE], F32, name="acc_%d_%d_%d" % (cg, n, m), tag="bank%d" % (2 * n + m)
+                    )
+            for g in range(PASSES):
+                h, gg = divmod(g, 2)
+                for n in range(n_tiles):
+                    cols = slice(n * N_TILE, (n + 1) * N_TILE)
+                    for m in range(ROW_TILES):
+                        nc.tensor.matmul_mx(
+                            out=acc[(n, m)][:],
+                            lhsT=x_codes[(m, h)][:, gg * P : (gg + 1) * P].bitcast(FP8X4),
+                            lhsT_scale=x_planes[(m, h)][:, gg * P : (gg + 1) * P],
+                            rhs=w_sb[(cg, g)][:, cols].bitcast(FP8X4),
+                            rhs_scale=w_planes[4 * g : P, c0 + n * N_TILE : c0 + (n + 1) * N_TILE],
+                            start=(g == 0),
+                            stop=(g == PASSES - 1),
+                        )
+                        if g == PASSES - 1:
+                            if m == 0:
+                                nc.vector.tensor_copy(out=staged[m][:, cols], in_=acc[(n, m)][:])
+                            else:
+                                nc.scalar.copy(out=staged[m][:, cols], in_=acc[(n, m)][:])
+            for m in range(ROW_TILES):
+                nc.sync.dma_start(out=out[m, :, c0 : c0 + width], in_=staged[m][:])

@@ -42,9 +42,9 @@ def tile_quantlinear_kernel(tc, x, w_words, w_scales, out):
             x_sb.append(x_m)
 
         for q in range(4):
-            nc.sync.dma_start(
-                out=w_planes[32 * q : 32 * q + 16, :].bitcast(I32),
-                in_=w_scales[:, 4 * q : 4 * q + 4, :].bitcast(I32),
+            nc.gpsimd.dma_start(
+                out=w_planes[32 * q : 32 * q + 16, :].bitcast(F32),
+                in_=w_scales[:, 4 * q : 4 * q + 4, :].bitcast(F32),
             )
 
         w_sb = {}

@@ -29,8 +29,11 @@ def tile_quantlinear_kernel(tc, x, w_words, w_scales, out):
         psum = ctx.enter_context(tc.psum_pool(name="psum", bufs=1))
         ctx.enter_context(tc.manual_schedule())
 
-        w_planes = keep.tile([P, OUT], U8, name="w_planes", align_bytes=64)
-        nc.vector.memset(w_planes[:].bitcast(I32), 0)
+        first_w = COLUMN_GROUPS[0][1]
+        planes_a = keep.tile([P, first_w], U8, name="planes_a", align_bytes=64)
+        planes_b = keep.tile([P, OUT - first_w], U8, name="planes_b", align_bytes=64)
+        nc.vector.memset(planes_a[:].bitcast(I32), 0)
+        nc.vector.memset(planes_b[:].bitcast(I32), 0)
 
         ident = keep.tile([P, P], F32, name="ident")
         make_identity(nc, ident[:])
@@ -42,9 +45,14 @@ def tile_quantlinear_kernel(tc, x, w_words, w_scales, out):
             x_sb.append(x_m)
 
         for q in range(4):
+            nc.sync.dma_start(
+                out=planes_a[32 * q : 32 * q + 16, :].bitcast(I32),
+                in_=w_scales[:, 4 * q : 4 * q + 4, 0:first_w].bitcast(I32),
+            )
+        for q in range(4):
             nc.gpsimd.dma_start(
-                out=w_planes[32 * q : 32 * q + 16, :].bitcast(F32),
-                in_=w_scales[:, 4 * q : 4 * q + 4, :].bitcast(F32),
+                out=planes_b[32 * q : 32 * q + 16, :].bitcast(F32),
+                in_=w_scales[:, 4 * q : 4 * q + 4, first_w:OUT].bitcast(F32),
             )
 
         w_sb = {}
@@ -91,6 +99,8 @@ def tile_quantlinear_kernel(tc, x, w_words, w_scales, out):
 
         for cg, (c0, width) in enumerate(COLUMN_GROUPS):
             n_tiles = width // N_TILE
+            planes = planes_a if cg == 0 else planes_b
+            p0 = c0 if cg == 0 else c0 - first_w
             acc = {}
             staged = []
             for m in range(ROW_TILES):
@@ -110,7 +120,7 @@ def tile_quantlinear_kernel(tc, x, w_words, w_scales, out):
                             lhsT=x_codes[(m, h)][:, gg * P : (gg + 1) * P].bitcast(FP8X4),
                             lhsT_scale=x_planes[(m, h)][:, gg * P : (gg + 1) * P],
                             rhs=w_sb[(cg, g)][:, cols].bitcast(FP8X4),
-                            rhs_scale=w_planes[4 * g : P, c0 + n * N_TILE : c0 + (n + 1) * N_TILE],
+                            rhs_scale=planes[4 * g : P, p0 + n * N_TILE : p0 + (n + 1) * N_TILE],
                             start=(g == 0),
                             stop=(g == PASSES - 1),
                         )

@@ -58,14 +58,19 @@ def tile_quantlinear_kernel(tc, x, w_words, w_scales, out):
         w_sb = {}
         for cg, (c0, width) in enumerate(COLUMN_GROUPS):
             for g in range(PASSES):
-                w_t = keep.tile([P, width], U32, name="w_%d_%d" % (cg, g), align_bytes=64)
-                src = w_words[g].rearrange("p n t -> p (n t)")[:, 4 * c0 : 4 * (c0 + width)]
-                nc.sync.dma_start(out=w_t[:].bitcast(I32), in_=src.bitcast(I32))
-                w_sb[(cg, g)] = w_t
+                pieces = 2 if (cg, g) == (0, 0) else 1
+                piece_w = width // pieces
+                piece_tiles = piece_w // N_TILE
+                for i in range(pieces):
+                    w_t = keep.tile([P, piece_w], U32, name="w_%d_%d_%d" % (cg, g, i), align_bytes=64)
+                    a = c0 + i * piece_w
+                    src = w_words[g].rearrange("p n t -> p (n t)")[:, 4 * a : 4 * (a + piece_w)]
+                    nc.sync.dma_start(out=w_t[:].bitcast(I32), in_=src.bitcast(I32))
+                    for j in range(piece_tiles):
+                        w_sb[(cg, g, i * piece_tiles + j)] = w_t[:, j * N_TILE : (j + 1) * N_TILE]
 
         x_codes = {}
         x_planes = {}
-        grouped = {}
         for m in range(ROW_TILES):
             x_words = x_sb[m][:].bitcast(F32)
             for h in range(2):
@@ -81,18 +86,13 @@ def tile_quantlinear_kernel(tc, x, w_words, w_scales, out):
                 grp = keep.tile([P, 4 * 2 * P], BF16, name="grouped_%d_%d" % (m, h), align_bytes=64)
                 dst = grp[:].bitcast(F32).rearrange("p (g c u) -> p g c u", g=2, c=P, u=2)
                 src = xt[:].rearrange("p g u c -> p g c u")
-                if h == 0:
-                    nc.vector.tensor_copy(out=dst, in_=src)
-                else:
-                    nc.scalar.copy(out=dst, in_=src)
-                grouped[(m, h)] = grp
-            for h in (1, 0):
+                nc.scalar.copy(out=dst, in_=src)
                 codes = keep.tile([P, 2 * P], U32, name="x_codes_%d_%d" % (m, h), align_bytes=64)
                 plane = keep.tile([P, 2 * P], U8, name="x_plane_%d_%d" % (m, h), align_bytes=64)
                 nc.vector.quantize_mx(
                     out=codes[:].bitcast(FP8X4),
                     scales=plane[:],
-                    in_=grouped[(m, h)][:],
+                    in_=grp[:],
                 )
                 x_codes[(m, h)] = codes
                 x_planes[(m, h)] = plane
@@ -119,7 +119,7 @@ def tile_quantlinear_kernel(tc, x, w_words, w_scales, out):
                             out=acc[(n, m)][:],
                             lhsT=x_codes[(m, h)][:, gg * P : (gg + 1) * P].bitcast(FP8X4),
                             lhsT_scale=x_planes[(m, h)][:, gg * P : (gg + 1) * P],
-                            rhs=w_sb[(cg, g)][:, cols].bitcast(FP8X4),
+                            rhs=w_sb[(cg, g, n)].bitcast(FP8X4),
                             rhs_scale=planes[4 * g : P, p0 + n * N_TILE : p0 + (n + 1) * N_TILE],
                             start=(g == 0),
                             stop=(g == PASSES - 1),

from contextlib import ExitStack

import concourse.mybir as mybir
from concourse.masks import make_identity

F32 = mybir.dt.float32
BF16 = mybir.dt.bfloat16
I32 = mybir.dt.int32
U32 = mybir.dt.uint32
U8 = mybir.dt.uint8
FP8X4 = mybir.dt.float8_e4m3fn_x4

P = 128
ROWS = 256
K = 2048
OUT = 5632
PASSES = 4
ROW_TILES = 2
N_TILE = 512
COLUMN_GROUPS = ((0, 2048), (2048, 2048), (4096, 1536))

FLOPS = 2 * ROWS * K * OUT


def tile_quantlinear_kernel(tc, x, w_words, w_scales, out):
    nc = tc.nc
    with ExitStack() as ctx:
        keep = ctx.enter_context(tc.tile_pool(name="keep", bufs=1))
        psum = ctx.enter_context(tc.psum_pool(name="psum", bufs=1))
        ctx.enter_context(tc.manual_schedule())

        first_w = COLUMN_GROUPS[0][1]
        planes_a = keep.tile([P, first_w], U8, name="planes_a", align_bytes=64)
        planes_b = keep.tile([P, OUT - first_w], U8, name="planes_b", align_bytes=64)
        nc.vector.memset(planes_a[:].bitcast(I32), 0)
        nc.vector.memset(planes_b[:].bitcast(I32), 0)

        ident = keep.tile([P, P], F32, name="ident")
        make_identity(nc, ident[:])

        x_sb = []
        for m in range(ROW_TILES):
            x_m = keep.tile([P, K], BF16, name="x_sb_%d" % m)
            nc.sync.dma_start(out=x_m[:], in_=x[m])
            x_sb.append(x_m)

        for q in range(4):
            nc.sync.dma_start(
                out=planes_a[32 * q : 32 * q + 16, :].bitcast(I32),
                in_=w_scales[:, 4 * q : 4 * q + 4, 0:first_w].bitcast(I32),
            )
        for q in range(4):
            nc.gpsimd.dma_start(
                out=planes_b[32 * q : 32 * q + 16, :].bitcast(F32),
                in_=w_scales[:, 4 * q : 4 * q + 4, first_w:OUT].bitcast(F32),
            )

        w_sb = {}
        for cg, (c0, width) in enumerate(COLUMN_GROUPS):
            for g in range(PASSES):
                pieces = 2 if (cg, g) == (0, 0) else 1
                piece_w = width // pieces
                piece_tiles = piece_w // N_TILE
                for i in range(pieces):
                    w_t = keep.tile([P, piece_w], U32, name="w_%d_%d_%d" % (cg, g, i), align_bytes=64)
                    a = c0 + i * piece_w
                    src = w_words[g].rearrange("p n t -> p (n t)")[:, 4 * a : 4 * (a + piece_w)]
                    nc.sync.dma_start(out=w_t[:].bitcast(I32), in_=src.bitcast(I32))
                    for j in range(piece_tiles):
                        w_sb[(cg, g, i * piece_tiles + j)] = w_t[:, j * N_TILE : (j + 1) * N_TILE]

        x_codes = {}
        x_planes = {}
        for m in range(ROW_TILES):
            x_words = x_sb[m][:].bitcast(F32)
            for h in range(2):
                xt = psum.tile([P, 2, 2, P], F32, name="xt_%d_%d" % (m, h), tag="bank%d" % (4 + 2 * m + h))
                for gg in range(2):
                    g = 2 * h + gg
                    for u in range(2):
                        nc.tensor.transpose(
                            xt[:, gg, u, :],
                            x_words[:, 256 * g + u : 256 * (g + 1) : 2],
                            ident[:],
                        )
                grp = keep.tile([P, 4 * 2 * P], BF16, name="grouped_%d_%d" % (m, h), align_bytes=64)
                dst = grp[:].bitcast(F32).rearrange("p (g c u) -> p g c u", g=2, c=P, u=2)
                src = xt[:].rearrange("p g u c -> p g c u")
                nc.scalar.copy(out=dst, in_=src)
                codes = keep.tile([P, 2 * P], U32, name="x_codes_%d_%d" % (m, h), align_bytes=64)
                plane = keep.tile([P, 2 * P], U8, name="x_plane_%d_%d" % (m, h), align_bytes=64)
                nc.vector.quantize_mx(
                    out=codes[:].bitcast(FP8X4),
                    scales=plane[:],
                    in_=grp[:],
                )
                x_codes[(m, h)] = codes
                x_planes[(m, h)] = plane

        for cg, (c0, width) in enumerate(COLUMN_GROUPS):
            n_tiles = width // N_TILE
            planes = planes_a if cg == 0 else planes_b
            p0 = c0 if cg == 0 else c0 - first_w
            acc = {}
            staged = []
            for m in range(ROW_TILES):
                staged.append(keep.tile([P, width], F32, name="staged_%d_%d" % (cg, m)))
            for n in range(n_tiles):
                for m in range(ROW_TILES):
                    acc[(n, m)] = psum.tile(
                        [P, N_TILE], F32, name="acc_%d_%d_%d" % (cg, n, m), tag="bank%d" % (2 * n + m)
                    )
            for g in range(PASSES):
                h, gg = divmod(g, 2)
                for n in range(n_tiles):
                    cols = slice(n * N_TILE, (n + 1) * N_TILE)
                    for m in range(ROW_TILES):
                        nc.tensor.matmul_mx(
                            out=acc[(n, m)][:],
                            lhsT=x_codes[(m, h)][:, gg * P : (gg + 1) * P].bitcast(FP8X4),
                            lhsT_scale=x_planes[(m, h)][:, gg * P : (gg + 1) * P],
                            rhs=w_sb[(cg, g, n)].bitcast(FP8X4),
                            rhs_scale=planes[4 * g : P, p0 + n * N_TILE : p0 + (n + 1) * N_TILE],
                            start=(g == 0),
                            stop=(g == PASSES - 1),
                        )
                        if g == PASSES - 1:
                            if m == 0:
                                nc.vector.tensor_copy(out=staged[m][:, cols], in_=acc[(n, m)][:])
                            else:
                                nc.scalar.copy(out=staged[m][:, cols], in_=acc[(n, m)][:])
            for m in range(ROW_TILES):
                nc.sync.dma_start(out=out[m, :, c0 : c0 + width], in_=staged[m][:])
